import numpy as np
import ml_dtypes


def mxq(x, axis, fmt="e4m3"):
    dtype, down = {"e4m3": (ml_dtypes.float8_e4m3fn, 7), "e5m2": (ml_dtypes.float8_e5m2, 14)}[fmt]
    v = np.moveaxis(np.asarray(x, np.float32).astype(ml_dtypes.bfloat16).astype(np.float64), axis, -1)
    blocks = v.reshape(v.shape[:-1] + (-1, 32))
    amax = np.abs(blocks).max(-1, keepdims=True)
    byte = np.maximum(np.where(amax > 0, np.frexp(amax)[1] - 1 + 127, 0) - down, 1)
    scale = np.exp2(byte - 127.0)
    codes = (blocks / scale).astype(np.float32).astype(dtype).astype(np.float64)
    return np.moveaxis((codes * scale).reshape(v.shape), -1, axis)


WIDE = False


def mx_kscale(k):
    if not WIDE:
        return np.ones(k)
    levels = np.array([10, -10, 5, -5, 0])
    if k % 512:
        return np.exp2(np.random.permutation(np.resize(levels, k // 32))).repeat(32)
    a = np.empty((k // 512, 16))
    for p in range(k // 512):
        a[p, :8] = np.random.permutation(np.resize(levels, 8))
        for g in range(8):
            far = levels[np.abs(levels - a[p, g]) >= 10]
            a[p, g + 8] = far[np.random.randint(len(far))]
    return np.exp2(a.ravel()).repeat(32)


BF16 = ml_dtypes.bfloat16


def bf(x):
    return np.asarray(x, np.float32).astype(BF16)


def f64(x):
    return np.asarray(x).astype(np.float64)


G, B, NF, T, I, R, H = 1, 4096, 512, 512, 512, 1024, 256


def setup_inputs():
    kf, kt, kr = mx_kscale(NF), mx_kscale(T), mx_kscale(R)
    return {"v": bf(np.random.standard_normal((B, NF)) * kf),
            "s": bf(np.random.standard_normal((B, T)) * kt),
            "Ca": bf(np.random.standard_normal((G, NF, R)) / np.sqrt(NF) / kf[:, None] * kr),
            "Cb": bf(np.random.standard_normal((G, T, R)) / np.sqrt(T) / kt[:, None]),
            "Cc": bf(np.random.standard_normal((G, R, H)) * 0.7 / np.sqrt(R) / kr[:, None])}


def reference(v, s, Ca, Cb, Cc):
    t3 = mxq(f64(v), 1, "e4m3") @ mxq(f64(Ca), 1, "e4m3")
    t4 = mxq(f64(s), 1, "e4m3") @ mxq(f64(Cb), 1, "e4m3")
    return mxq(t3 * t4, 2, "e4m3") @ mxq(f64(Cc), 1, "e4m3")

@@ -1,0 +1,335 @@
+from contextlib import ExitStack
+
+import concourse.mybir as mybir
+from concourse.masks import make_identity
+
+F32 = mybir.dt.float32
+BF16 = mybir.dt.bfloat16
+U8 = mybir.dt.uint8
+U32 = mybir.dt.uint32
+FP8X4 = mybir.dt.float8_e4m3fn_x4
+
+P = 128
+B, K, R, H = 4096, 512, 1024, 256
+NSUB = B // P
+FLOPS = 2 * B * (2 * K * R + R * H)
+NPH = 16
+VSHARE = 352
+SPEC = {"banks":[3,3,2],"head":{"P":[["T",0],["T",1],["A",0,0],["A",0,1]],"S":[["RW","a",0],["Xv",0],["RW","b",0],["Xs",0],["Xv",1],["Xs",1],["C",0,0],["C",0,1]],"V":[["RW","a",0],["RW","b",0],["QW","a",0],["QX",0],["QW","b",0]]},"phase":{"P":[["T",{"d":2}],["A",{"d":0},2],["B",{"d":0},0],["A",{"d":0},3],["B",{"d":0},1],["S3",{"d":-4}],["A",{"d":1},0],["B",{"d":0},2],["A",{"d":1},1],["B",{"d":0},3]],"S":[["Xv",{"d":2}],["Xs",{"d":2}],["C",{"d":0},2],["C",{"d":0},3],["O",{"d":-4}],["C",{"d":1},0],["C",{"d":1},1]],"V":[["M",{"d":0},0],["QX",{"d":2}],["M",{"d":0},1],["M",{"d":0},2],["QP",{"d":-2}],["M",{"d":0},3]]},"phase_special":{"0":{"P":[["B",0,0],["B",0,1],["A",0,2],["A",0,3],["T",2],["B",0,2],["B",0,3],["A",1,0],["A",1,1]],"S":[["RW","a",1],["C",0,2],["C",0,3],["Xv",2],["Xs",2],["RW","b",1],["C",1,0],["C",1,1]],"V":[["QX",1],["RW","a",1],["M",0,0],["M",0,1],["QW","a",1],["RW","b",1],["M",0,2],["QX",2],["QW","b",1],["M",0,3]]},"1":{"V":[["M",{"d":0},0],["QX",{"d":2}],["M",{"d":0},1],["RC"],["M",{"d":0},2],["M",{"d":0},3]]},"3":{"V":[["M",{"d":0},0],["QX",{"d":2}],["M",{"d":0},1],["QP",{"d":-2}],["M",{"d":0},2],["QC"],["M",{"d":0},3]]},"14":{"P":[["A",14,2],["B",14,0],["A",14,3],["B",14,1],["S3",10],["A",15,0],["B",14,2],["A",15,1],["B",14,3],["S3",11],["A",15,2],["B",15,0],["A",15,3],["S3",12],["B",15,1],["B",15,2],["B",15,3],["S3",13],["S3",14],["S3h",2],["S3h",3]],"S":[["C",14,2],["C",14,3],["O",10],["C",15,0],["C",15,1],["O",11],["C",15,2],["O",12],["C",15,3],["O",13],["O",14],["Oh",2]],"V":[["M",14,0],["QP",12],["M",14,1],["QP",13],["M",14,2],["M",14,3],["M",15,0],["M",15,1],["QP",14],["QPa",15],["M",15,2],["M",15,3],["QPc",15],["QPd",15],["Ohv",3]]},"15":{"P":[["NOP"]],"S":[["NOP"]],"V":[["NOP"]]}},"tail":{"P":[],"S":[],"V":[]},"vshare":[352,352,1],"pbf":4,"pq":6,"dma":[["w","a",0],["x","v",0,0,2],["w","b",0],["x","s",0,0,2],["x","v",0,2,4],["x","s",0,2,4],["x","v",1,0,2],["x","s",1,0,2],["w","a",1],["w","b",1],["x","v",1,2,4],["x","s",1,2,4],["c"]],"t3":3}
+NA = 3
+NB = 3
+NM = 2
+
+
+def tile_vnclcell_pa_t_kernel(tc, v, s, Ca, Cb, Cc, out):
+    nc = tc.nc
+    with ExitStack() as ctx:
+        keep = ctx.enter_context(tc.tile_pool(name="keep", bufs=1))
+        ring = ctx.enter_context(tc.tile_pool(name="ring", bufs=2))
+        psum = ctx.enter_context(tc.psum_pool(name="psum", bufs=1))
+        ctx.enter_context(tc.manual_schedule())
+
+        ident = keep.tile([P, P], F32, name="ident")
+        make_identity(nc, ident[:])
+
+        rows = {"v": v.rearrange("(p n) k -> p (n k)", n=NSUB), "s": s.rearrange("(p n) k -> p (n k)", n=NSUB)}
+        out_rows = out.rearrange("g (p n) h -> (g p) (n h)", n=NSUB)
+        wsrc = {"a": Ca, "b": Cb}
+
+        x_in = {}
+        for c in range(8):
+            for x in "vs":
+                x_in[x, c] = keep.tile([P, 4 * K], BF16, name="x_%s%d" % (x, c))
+        w_raw = {}
+        w_q = {}
+        w_s = {}
+        for w in "ab":
+            for g in range(2):
+                w_raw[w, g] = keep.tile([P, 4, 512], BF16, name="raw_%s%d" % (w, g))
+            w_q[w] = keep.tile([P, R], U32, name="wq_" + w, align_bytes=64)
+            w_s[w] = keep.tile([P, R], U8, name="ws_" + w, align_bytes=64)
+        c_raw = keep.tile([P, 8, H], BF16, name="raw_c")
+        c_q = keep.tile([P, 2 * H], U32, name="cq", align_bytes=64)
+        c_s = keep.tile([P, 2 * H], U8, name="cs", align_bytes=64)
+
+        def load_x(x, c, lo, hi):
+            nc.sync.dma_start(out=x_in[x, c][:, lo * K:hi * K], in_=rows[x][:, (4 * c + lo) * K:(4 * c + hi) * K])
+
+        def load_w(w, g):
+            nc.sync.dma_start(out=w_raw[w, g][:], in_=wsrc[w][0, :, 512 * g:512 * g + 512].rearrange("(p j) c -> p j c", j=4))
+
+        for item in SPEC["dma"]:
+            if item[0] == "w":
+                load_w(item[1], item[2])
+            elif item[0] == "x":
+                load_x(item[1], item[2], item[3], item[4])
+            else:
+                nc.sync.dma_start(out=c_raw[:, 0:4, :], in_=Cc[0, 0:512, :].rearrange("(p j) h -> p j h", j=4))
+                nc.sync.dma_start(out=c_raw[:, 4:8, :], in_=Cc[0, 512:1024, :].rearrange("(p j) h -> p j h", j=4))
+        for c in range(2, 8):
+            load_x("v", c, 0, 4)
+            load_x("s", c, 0, 4)
+
+        def regroup(copy, dst, src):
+            copy(out=dst.rearrange("p (c i t) -> p c t i", i=4, t=4), in_=src.rearrange("p t (c i) -> p c t i", i=4))
+
+        grp = {}
+
+        def w_regroup(w, g):
+            grp[w, g] = ring.tile([P, 2048], BF16, name="grp", tag="grp", bufs=3, align_bytes=64)
+            vs = SPEC["vshare"][g] // 4
+            dst = grp[w, g][:].rearrange("p (t m j) -> p m j t", t=4, j=4)
+            src = w_raw[w, g][:].rearrange("p j (m t) -> p m j t", t=4)
+            nc.vector.tensor_copy(out=dst[:, 0:vs], in_=src[:, 0:vs])
+            nc.scalar.copy(out=dst[:, vs:P], in_=src[:, vs:P])
+
+        def w_quant(w, g):
+            nc.vector.quantize_mx(out=w_q[w][:, 512 * g:512 * g + 512].bitcast(FP8X4), scales=w_s[w][:, 512 * g:512 * g + 512],
+                                  in_=grp[w, g][:])
+
+        def c_regroup(copy):
+            grp["c"] = ring.tile([P, 2048], BF16, name="grp", tag="grp", bufs=3, align_bytes=64)
+            regroup(nc.vector.tensor_copy, grp["c"][:, 0:1024], c_raw[:, 0:4, :])
+            regroup(nc.vector.tensor_copy if SPEC["vshare"][2] else nc.scalar.copy, grp["c"][:, 1024:2048], c_raw[:, 4:8, :])
+
+        def c_quant():
+            nc.vector.quantize_mx(out=c_q[:].bitcast(FP8X4), scales=c_s[:], in_=grp["c"][:])
+
+        tb = {}
+        xg = {}
+        xq = {}
+        xs = {}
+
+        def T(t):
+            c, hp = divmod(t, 2)
+            for x in "vs":
+                tb[x, t] = psum.tile([P, 512], F32, name="tb", tag="m", bufs=NM)
+                words = x_in[x, c][:].bitcast(F32)
+                for u in range(2):
+                    for i in range(2):
+                        nc.tensor.transpose(tb[x, t][:, 256 * u + 128 * i:256 * u + 128 * i + 128],
+                                            words[:, (2 * hp + i) * 256 + u:(2 * hp + i + 1) * 256:2], ident[:])
+
+        def X(t, x, copy):
+            if x == "v":
+                xg[t] = ring.tile([P, 2048], BF16, name="xg", tag="xg", bufs=3, align_bytes=64)
+            o = 0 if x == "v" else 512
+            copy(out=xg[t][:].bitcast(F32)[:, o:o + 512].rearrange("p (c u) -> p c u", u=2),
+                 in_=tb[x, t][:].rearrange("p (u c) -> p c u", u=2))
+
+        def QX(t):
+            xq[t] = ring.tile([P, 512], U32, name="xq", tag="xq", bufs=6, align_bytes=64)
+            xs[t] = ring.tile([P, 512], U8, name="xs", tag="xs", bufs=6, align_bytes=64)
+            nc.vector.quantize_mx(out=xq[t][:].bitcast(FP8X4), scales=xs[t][:], in_=xg[t][:])
+
+        bank = {}
+        t3 = {}
+        pbf = {}
+        pq = {}
+        ps = {}
+
+        def U(f, nl, which):
+            c, g = divmod(f, 2)
+            t, i = 2 * c + nl // 2, nl % 2
+            if which == "a":
+                bank["a", f, nl] = psum.tile([P, 512], F32, name="bka", tag="a", bufs=NA)
+                for jj in range(2):
+                    m = (4 * g + 2 * i + jj) * P
+                    nc.tensor.matmul_mx(out=bank["a", f, nl][:, jj * 256:(jj + 1) * 256],
+                                        lhsT=w_q["a"][:, m:m + P].bitcast(FP8X4), lhsT_scale=w_s["a"][:, m:m + P],
+                                        rhs=xq[t][:, 0:256].bitcast(FP8X4), rhs_scale=xs[t][:, 0:256],
+                                        start=True, stop=True)
+                return
+            for w, o, nb in (("b", 256, NB),):
+                bank[w, f, nl] = psum.tile([P, 512], F32, name="bk" + w, tag=w, bufs=nb)
+                for j in range(4):
+                    m = (4 * g + j) * P
+                    n = o + i * P
+                    nc.tensor.matmul_mx(out=bank[w, f, nl][:, j * P:(j + 1) * P],
+                                        lhsT=w_q[w][:, m:m + P].bitcast(FP8X4), lhsT_scale=w_s[w][:, m:m + P],
+                                        rhs=xq[t][:, n:n + P].bitcast(FP8X4), rhs_scale=xs[t][:, n:n + P],
+                                        start=True, stop=True)
+
+        def C(f, nl):
+            if nl % 2 == 0:
+                t3[f, nl // 2] = ring.tile([P, 2, 256, 2], F32, name="t3", tag="t3", bufs=SPEC.get("t3", 3))
+            nc.scalar.copy(out=t3[f, nl // 2][:, nl % 2, :, :], in_=bank["a", f, nl][:].rearrange("p (e w) -> p w e", e=2))
+
+        def M(f, nl):
+            if nl == 0:
+                pbf[f] = ring.tile([P, 2048], BF16, name="pbf", tag="pbf", bufs=SPEC.get("pbf", 3), align_bytes=64)
+            nc.vector.tensor_tensor(out=pbf[f][:, 512 * nl:512 * nl + 512].rearrange("p (w h e) -> p w h e", h=2, e=2),
+                                    in0=bank["b", f, nl][:].rearrange("p (h e w) -> p w h e", h=2, e=2),
+                                    in1=t3[f, nl // 2][:, :, (nl % 2) * P:(nl % 2 + 1) * P, :].rearrange("p h w e -> p w h e"),
+                                    op=mybir.AluOpType.mult)
+
+        def QP(f, lo=0, hi=4):
+            if lo == 0:
+                pq[f] = ring.tile([P, 512], U32, name="pq", tag="pq", bufs=SPEC.get("pq", 6), align_bytes=64)
+                ps[f] = ring.tile([P, 512], U8, name="ps", tag="ps", bufs=SPEC.get("pq", 6), align_bytes=64)
+            nc.vector.quantize_mx(out=pq[f][:, P * lo:P * hi].bitcast(FP8X4), scales=ps[f][:, P * lo:P * hi],
+                                  in_=pbf[f][:, 512 * lo:512 * hi])
+
+        ob = {}
+        osb = {}
+
+        def S3(c, lo, hi, tag="m", nb=NM):
+            ob[c, lo] = psum.tile([P, 512], F32, name="ob", tag=tag, bufs=nb)
+            for nl in range(lo, hi):
+                for g in range(2):
+                    nc.tensor.matmul_mx(out=ob[c, lo][:, (nl - lo) * H:(nl - lo + 1) * H],
+                                        lhsT=pq[2 * c + g][:, nl * P:(nl + 1) * P].bitcast(FP8X4),
+                                        lhsT_scale=ps[2 * c + g][:, nl * P:(nl + 1) * P],
+                                        rhs=c_q[:, g * H:(g + 1) * H].bitcast(FP8X4), rhs_scale=c_s[:, g * H:(g + 1) * H],
+                                        start=(g == 0), stop=(g == 1))
+
+        def O(c, lo, hi, copy):
+            w = (hi - lo) * H
+            osb[c, lo] = ring.tile([P, 512], F32, name="osb", tag="osb", bufs=4)
+            copy(out=osb[c, lo][:, 0:w], in_=ob[c, lo][:, 0:w])
+            nc.sync.dma_start(out=out_rows[:, (4 * c + lo) * H:(4 * c + hi) * H], in_=osb[c, lo][:, 0:w])
+
+        vcopy = nc.vector.tensor_copy
+        scopy = nc.scalar.copy
+
+        ops = {}
+        def add(key, eng, fn, pre):
+            ops[key] = (eng, fn, pre)
+        for w in "ab":
+            for g in range(2):
+                add(("RW", w, g), "VS", (lambda w=w, g=g: w_regroup(w, g)), [])
+                add(("QW", w, g), "V", (lambda w=w, g=g: w_quant(w, g)), [("RW", w, g)])
+        add(("RC",), "V", (lambda: c_regroup(vcopy)), [])
+        add(("QC",), "V", c_quant, [("RC",)])
+        for t in range(16):
+            add(("T", t), "P", (lambda t=t: T(t)), [])
+            add(("Xv", t), "S", (lambda t=t: X(t, "v", scopy)), [("T", t)])
+            add(("Xs", t), "S", (lambda t=t: X(t, "s", scopy)), [("T", t), ("Xv", t)])
+            add(("QX", t), "V", (lambda t=t: QX(t)), [("Xs", t)])
+        for f in range(16):
+            c, g = divmod(f, 2)
+            for nl in range(4):
+                t = 2 * c + nl // 2
+                add(("A", f, nl), "P", (lambda f=f, nl=nl: U(f, nl, "a")), [("QX", t), ("QW", "a", g)])
+                add(("B", f, nl), "P", (lambda f=f, nl=nl: U(f, nl, "b")), [("QX", t), ("QW", "b", g)])
+                add(("C", f, nl), "S", (lambda f=f, nl=nl: C(f, nl)), [("A", f, nl)])
+                add(("M", f, nl), "V", (lambda f=f, nl=nl: M(f, nl)), [("C", f, 2 * (nl // 2)), ("C", f, 2 * (nl // 2) + 1), ("B", f, nl)] + ([("M", f, nl - 1)] if nl else []))
+            add(("QP", f), "V", (lambda f=f: QP(f)), [("M", f, 3)])
+            add(("QPa", f), "V", (lambda f=f: QP(f, 0, 2)), [("M", f, 1)])
+            add(("QPb", f), "V", (lambda f=f: QP(f, 2, 4)), [("M", f, 3), ("QPa", f)])
+            add(("QPc", f), "V", (lambda f=f: QP(f, 2, 3)), [("M", f, 2), ("QPa", f)])
+            add(("QPd", f), "V", (lambda f=f: QP(f, 3, 4)), [("M", f, 3), ("QPc", f)])
+        for q in range(16):
+            c = q // 2
+            add(("S3", q), "P", (lambda q=q: S3(q // 2, 2 * (q % 2), 2 * (q % 2) + 2)), [("QPx", 2 * c, q % 2), ("QPx", 2 * c + 1, q % 2), ("QC",)])
+            add(("O", q), "S", (lambda q=q: O(q // 2, 2 * (q % 2), 2 * (q % 2) + 2, scopy)), [("S3", q)])
+            add(("Ov", q), "V", (lambda q=q: O(q // 2, 2 * (q % 2), 2 * (q % 2) + 2, vcopy)), [("S3", q)])
+        for nl in (2, 3):
+            add(("S3h", nl), "P", (lambda nl=nl: S3(7, nl, nl + 1)), [("QPx", 14, 1), ("QPy", 15, nl), ("QC",)])
+            add(("Oh", nl), "S", (lambda nl=nl: O(7, nl, nl + 1, scopy)), [("S3h", nl)])
+            add(("Ohv", nl), "V", (lambda nl=nl: O(7, nl, nl + 1, vcopy)), [("S3h", nl)])
+
+        def expand(seq, f):
+            res = []
+            for item in seq:
+                nm, args = item[0], item[1:]
+                key = tuple([nm] + [(f + a["d"] if isinstance(a, dict) else a) for a in args])
+                res.append(key)
+            return res
+
+        queues = {"P": [], "S": [], "V": []}
+        for e in "PSV":
+            for key in SPEC["head"][e]:
+                queues[e].append(tuple(key))
+        for f in range(16):
+            for e in "PSV":
+                spec = SPEC["phase_special"].get(str(f), {}).get(e) or SPEC["phase"][e]
+                for key in expand(spec, f):
+                    if key[0] == "NOP": continue
+                    if key[0] in ("T", "Xv", "Xs", "QX") and not (0 <= key[1] < 16): continue
+                    if key[0] in ("S3", "O", "Ov") and not (0 <= key[1] < 16): continue
+                    if key[0] in ("QP", "A", "B", "C", "M") and not (0 <= key[1] < 16): continue
+                    queues[e].append(key)
+        for e in "PSV":
+            for key in SPEC["tail"][e]:
+                queues[e].append(tuple(key))
+        done = set()
+
+        def sat(p):
+            if p[0] == "QPx":
+                return ("QP", p[1]) in done or (("QPa", p[1]) in done if p[2] == 0 else (("QPb", p[1]) in done or ("QPd", p[1]) in done))
+            if p[0] == "QPy":
+                return ("QP", p[1]) in done or ("QPb", p[1]) in done or (("QPc", p[1]) in done if p[2] == 2 else ("QPd", p[1]) in done)
+            if p[0] == "Oany":
+                return ("O", p[1]) in done or ("Ov", p[1]) in done
+            if p[0] == "Ohany":
+                return ("Oh", p[1]) in done or ("Ohv", p[1]) in done
+            return p in done
+
+        m_readers = []
+        grp_users = []
+
+        def reuse(key):
+            k = key[0]
+            res = []
+            if k in ("A", "B", "C"):
+                n = 4 * key[1] + key[2]
+                back = {"A": NA, "B": NB, "C": 2 * SPEC.get("t3", 3) - 1}[k]
+                if k == "C" and n % 2 == 1:
+                    back = n + 1
+                if n - back >= 0:
+                    res.append(({"A": "C", "B": "M", "C": "M"}[k], (n - back) // 4, (n - back) % 4))
+            if k in ("T", "S3", "S3h"):
+                need = 2 if k == "T" else 1
+                for i in range(need):
+                    j = len(m_readers) + i - NM
+                    if j >= 0:
+                        res.append(m_readers[j] if j < len(m_readers) else ("never",))
+            if k == "Xv" and key[1] >= 3:
+                res.append(("QX", key[1] - 3))
+            if k == "QX" and key[1] >= 6:
+                t = key[1] - 6
+                res.append(("B", 2 * (t // 2) + 1, 2 * (t % 2) + 1))
+            if k == "M" and key[2] == 0 and key[1] >= SPEC.get("pbf", 3):
+                res.append(("QPx", key[1] - SPEC.get("pbf", 3), 1))
+            if k in ("QP", "QPa") and key[1] >= SPEC.get("pq", 6):
+                res.append(("S3", 2 * ((key[1] - SPEC.get("pq", 6)) // 2) + 1))
+            if k in ("RW", "RC") and len(grp_users) >= 3:
+                res.append(grp_users[len(grp_users) - 3])
+            return res
+
+        def emitted(key):
+            k = key[0]
+            if k == "T":
+                m_readers.append(("Xv", key[1]))
+                m_readers.append(("Xs", key[1]))
+            if k == "S3":
+                m_readers.append(("Oany", key[1]))
+            if k == "S3h":
+                m_readers.append(("Ohany", key[1]))
+            if k == "RW":
+                grp_users.append(("QW", key[1], key[2]))
+            if k == "RC":
+                grp_users.append(("QC",))
+            done.add(key)
+
+        pos = {"P": 0, "S": 0, "V": 0}
+        while any(pos[e] < len(queues[e]) for e in "PSV"):
+            prog = False
+            for e in "PSV":
+                if pos[e] >= len(queues[e]):
+                    continue
+                key = queues[e][pos[e]]
+                eng, fn, prq = ops[key]
+                if not all(sat(p) for p in list(prq) + reuse(key)):
+                    continue
+                if key[0] == "RW" or (key[0] == "RC" and not SPEC["vshare"][2]):
+                    other = "S" if e == "V" else "V"
+                    if not (pos[other] < len(queues[other]) and queues[other][pos[other]] == key):
+                        continue
+                    pos[other] += 1
+                fn()
+                emitted(key)
+                pos[e] += 1
+                prog = True
+            assert prog, "the three orders cannot be merged"

@@ -19,6 +19,8 @@ SPEC = {"banks":[3,3,2],"head":{"P":[["T",0],["T",1],["A",0,0],["A",0,1]],"S":[[
 NA = 3
 NB = 3
 NM = 2
+PERM = "vs"
+PFIRST = 3
 
 
 def tile_vnclcell_pa_t_kernel(tc, v, s, Ca, Cb, Cc, out):
@@ -100,6 +102,15 @@ def tile_vnclcell_pa_t_kernel(tc, v, s, Ca, Cb, Cc, out):
         xq = {}
         xs = {}
 
+        xp = {}
+
+        def PW(t):
+            c, hp = divmod(t, 2)
+            for x in PERM:
+                xp[x, t] = ring.tile([P, 1024], BF16, name="xp" + x, tag="xp" + x, bufs=3, align_bytes=64)
+                nc.gpsimd.tensor_copy(out=xp[x, t][:].bitcast(U32).rearrange("p (i u q) -> p i u q", i=2, u=2),
+                                      in_=x_in[x, c][:, 1024 * hp:1024 * hp + 1024].bitcast(U32).rearrange("p (i q u) -> p i u q", i=2, u=2))
+
         def T(t):
             c, hp = divmod(t, 2)
             for x in "vs":
@@ -107,8 +118,11 @@ def tile_vnclcell_pa_t_kernel(tc, v, s, Ca, Cb, Cc, out):
                 words = x_in[x, c][:].bitcast(F32)
                 for u in range(2):
                     for i in range(2):
-                        nc.tensor.transpose(tb[x, t][:, 256 * u + 128 * i:256 * u + 128 * i + 128],
-                                            words[:, (2 * hp + i) * 256 + u:(2 * hp + i + 1) * 256:2], ident[:])
+                        if (x, t) in xp:
+                            w = xp[x, t][:].bitcast(F32)[:, 256 * i + 128 * u:256 * i + 128 * u + 128]
+                        else:
+                            w = words[:, (2 * hp + i) * 256 + u:(2 * hp + i + 1) * 256:2]
+                        nc.tensor.transpose(tb[x, t][:, 256 * u + 128 * i:256 * u + 128 * i + 128], w, ident[:])
 
         def X(t, x, copy):
             if x == "v":
@@ -121,6 +135,9 @@ def tile_vnclcell_pa_t_kernel(tc, v, s, Ca, Cb, Cc, out):
             xq[t] = ring.tile([P, 512], U32, name="xq", tag="xq", bufs=6, align_bytes=64)
             xs[t] = ring.tile([P, 512], U8, name="xs", tag="xs", bufs=6, align_bytes=64)
             nc.vector.quantize_mx(out=xq[t][:].bitcast(FP8X4), scales=xs[t][:], in_=xg[t][:])
+
+        for t in range(PFIRST, PFIRST + 3):
+            PW(t)
 
         bank = {}
         t3 = {}
@@ -202,7 +219,7 @@ def tile_vnclcell_pa_t_kernel(tc, v, s, Ca, Cb, Cc, out):
         add(("RC",), "V", (lambda: c_regroup(vcopy)), [])
         add(("QC",), "V", c_quant, [("RC",)])
         for t in range(16):
-            add(("T", t), "P", (lambda t=t: T(t)), [])
+            add(("T", t), "P", (lambda t=t: (T(t), PW(t + 3) if PFIRST <= t <= 12 else 0)), [])
             add(("Xv", t), "S", (lambda t=t: X(t, "v", scopy)), [("T", t)])
             add(("Xs", t), "S", (lambda t=t: X(t, "s", scopy)), [("T", t), ("Xv", t)])
             add(("QX", t), "V", (lambda t=t: QX(t)), [("Xs", t)])

@@ -15,12 +15,12 @@ NSUB = B // P
 FLOPS = 2 * B * (2 * K * R + R * H)
 NPH = 16
 VSHARE = 352
-SPEC = {"banks":[3,3,2],"head":{"P":[["T",0],["T",1],["A",0,0],["A",0,1]],"S":[["RW","a",0],["Xv",0],["RW","b",0],["Xs",0],["Xv",1],["Xs",1],["C",0,0],["C",0,1]],"V":[["RW","a",0],["RW","b",0],["QW","a",0],["QX",0],["QW","b",0]]},"phase":{"P":[["T",{"d":2}],["A",{"d":0},2],["B",{"d":0},0],["A",{"d":0},3],["B",{"d":0},1],["S3",{"d":-4}],["A",{"d":1},0],["B",{"d":0},2],["A",{"d":1},1],["B",{"d":0},3]],"S":[["Xv",{"d":2}],["Xs",{"d":2}],["C",{"d":0},2],["C",{"d":0},3],["O",{"d":-4}],["C",{"d":1},0],["C",{"d":1},1]],"V":[["M",{"d":0},0],["QX",{"d":2}],["M",{"d":0},1],["M",{"d":0},2],["QP",{"d":-2}],["M",{"d":0},3]]},"phase_special":{"0":{"P":[["B",0,0],["B",0,1],["A",0,2],["A",0,3],["T",2],["B",0,2],["B",0,3],["A",1,0],["A",1,1]],"S":[["RW","a",1],["C",0,2],["C",0,3],["Xv",2],["Xs",2],["RW","b",1],["C",1,0],["C",1,1]],"V":[["QX",1],["RW","a",1],["M",0,0],["M",0,1],["QW","a",1],["RW","b",1],["M",0,2],["QX",2],["QW","b",1],["M",0,3]]},"1":{"V":[["M",{"d":0},0],["QX",{"d":2}],["M",{"d":0},1],["RC"],["M",{"d":0},2],["M",{"d":0},3]]},"3":{"V":[["M",{"d":0},0],["QX",{"d":2}],["M",{"d":0},1],["QP",{"d":-2}],["M",{"d":0},2],["QC"],["M",{"d":0},3]]},"14":{"P":[["A",14,2],["B",14,0],["A",14,3],["B",14,1],["S3",10],["A",15,0],["B",14,2],["A",15,1],["B",14,3],["S3",11],["A",15,2],["B",15,0],["A",15,3],["S3",12],["B",15,1],["B",15,2],["B",15,3],["S3",13],["S3",14],["S3h",2],["S3h",3]],"S":[["C",14,2],["C",14,3],["O",10],["C",15,0],["C",15,1],["O",11],["C",15,2],["O",12],["C",15,3],["O",13],["O",14],["Oh",2]],"V":[["M",14,0],["QP",12],["M",14,1],["QP",13],["M",14,2],["M",14,3],["M",15,0],["M",15,1],["QP",14],["QPa",15],["M",15,2],["M",15,3],["QPc",15],["QPd",15],["Ohv",3]]},"15":{"P":[["NOP"]],"S":[["NOP"]],"V":[["NOP"]]}},"tail":{"P":[],"S":[],"V":[]},"vshare":[352,352,1],"pbf":4,"pq":6,"dma":[["w","a",0],["x","v",0,0,2],["w","b",0],["x","s",0,0,2],["x","v",0,2,4],["x","s",0,2,4],["x","v",1,0,2],["x","s",1,0,2],["w","a",1],["w","b",1],["x","v",1,2,4],["x","s",1,2,4],["c"]],"t3":3}
+SPEC = {"banks":[3,3,2],"head":{"P":[["T",0],["T",1],["A",0,0],["A",0,1]],"S":[["RW","a",0],["Xv",0],["RW","b",0],["Xs",0],["Xv",1],["Xs",1],["C",0,0],["C",0,1]],"V":[["RW","a",0],["RW","b",0],["QW","a",0],["QX",0],["QW","b",0]]},"phase":{"P":[["T",{"d":2}],["A",{"d":0},2],["B",{"d":0},0],["A",{"d":0},3],["B",{"d":0},1],["S3",{"d":-4}],["A",{"d":1},0],["B",{"d":0},2],["A",{"d":1},1],["B",{"d":0},3]],"S":[["Xv",{"d":2}],["Xs",{"d":2}],["C",{"d":0},2],["C",{"d":0},3],["O",{"d":-4}],["C",{"d":1},0],["C",{"d":1},1]],"V":[["M",{"d":0},0],["QP",{"d":-2}],["QX",{"d":2}],["M",{"d":0},1],["M",{"d":0},2],["M",{"d":0},3]]},"phase_special":{"0":{"P":[["B",0,0],["B",0,1],["A",0,2],["A",0,3],["T",2],["B",0,2],["B",0,3],["A",1,0],["A",1,1]],"S":[["RW","a",1],["C",0,2],["C",0,3],["Xv",2],["Xs",2],["RW","b",1],["C",1,0],["C",1,1]],"V":[["QX",1],["RW","a",1],["M",0,0],["M",0,1],["QW","a",1],["RW","b",1],["M",0,2],["QX",2],["QW","b",1],["M",0,3]]},"1":{"V":[["M",{"d":0},0],["QX",{"d":2}],["M",{"d":0},1],["RC"],["M",{"d":0},2],["M",{"d":0},3]]},"3":{"V":[["M",{"d":0},0],["QP",{"d":-2}],["QX",{"d":2}],["M",{"d":0},1],["M",{"d":0},2],["QC"],["M",{"d":0},3]]},"14":{"P":[["A",14,2],["B",14,0],["A",14,3],["B",14,1],["S3",10],["A",15,0],["B",14,2],["A",15,1],["B",14,3],["S3",11],["A",15,2],["B",15,0],["A",15,3],["S3",12],["B",15,1],["B",15,2],["B",15,3],["S3",13],["S3",14],["S3h",2],["S3h",3]],"S":[["C",14,2],["C",14,3],["O",10],["C",15,0],["C",15,1],["O",11],["C",15,2],["O",12],["C",15,3],["O",13],["O",14],["Oh",2]],"V":[["M",14,0],["QP",12],["M",14,1],["QP",13],["M",14,2],["M",14,3],["M",15,0],["M",15,1],["QP",14],["QPa",15],["M",15,2],["M",15,3],["QPc",15],["QPd",15],["Ohv",3]]},"15":{"P":[["NOP"]],"S":[["NOP"]],"V":[["NOP"]]}},"tail":{"P":[],"S":[],"V":[]},"vshare":[352,352,1],"pbf":4,"pq":6,"dma":[["w","a",0],["x","v",0,0,2],["w","b",0],["x","s",0,0,2],["x","v",0,2,4],["x","s",0,2,4],["x","v",1,0,2],["x","s",1,0,2],["w","a",1],["w","b",1],["x","v",1,2,4],["x","s",1,2,4],["c"]],"t3":3}
 NA = 3
 NB = 3
 NM = 2
 PERM = "vs"
-PFIRST = 3
+PFIRST = 6
 
 
 def tile_vnclcell_pa_t_kernel(tc, v, s, Ca, Cb, Cc, out):

@@ -8,19 +8,19 @@ BF16 = mybir.dt.bfloat16
 U8 = mybir.dt.uint8
 U32 = mybir.dt.uint32
 FP8X4 = mybir.dt.float8_e4m3fn_x4
+MULT = mybir.AluOpType.mult
 
 P = 128
 B, K, R, H = 4096, 512, 1024, 256
-NSUB = B // P
+ROWS = B // P
+HALF = 512
 FLOPS = 2 * B * (2 * K * R + R * H)
-NPH = 16
-VSHARE = 352
-SPEC = {"banks":[3,3,2],"head":{"P":[["T",0],["T",1],["A",0,0],["A",0,1]],"S":[["RW","a",0],["Xv",0],["RW","b",0],["Xs",0],["Xv",1],["Xs",1],["C",0,0],["C",0,1]],"V":[["RW","a",0],["RW","b",0],["QW","a",0],["QX",0],["QW","b",0]]},"phase":{"P":[["T",{"d":2}],["A",{"d":0},2],["B",{"d":0},0],["A",{"d":0},3],["B",{"d":0},1],["S3",{"d":-4}],["A",{"d":1},0],["B",{"d":0},2],["A",{"d":1},1],["B",{"d":0},3]],"S":[["Xv",{"d":2}],["Xs",{"d":2}],["C",{"d":0},2],["C",{"d":0},3],["O",{"d":-4}],["C",{"d":1},0],["C",{"d":1},1]],"V":[["M",{"d":0},0],["QP",{"d":-2}],["QX",{"d":2}],["M",{"d":0},1],["M",{"d":0},2],["M",{"d":0},3]]},"phase_special":{"0":{"P":[["B",0,0],["B",0,1],["A",0,2],["A",0,3],["T",2],["B",0,2],["B",0,3],["A",1,0],["A",1,1]],"S":[["RW","a",1],["C",0,2],["C",0,3],["Xv",2],["Xs",2],["RW","b",1],["C",1,0],["C",1,1]],"V":[["QX",1],["RW","a",1],["M",0,0],["M",0,1],["QW","a",1],["RW","b",1],["M",0,2],["QX",2],["QW","b",1],["M",0,3]]},"1":{"V":[["M",{"d":0},0],["QX",{"d":2}],["M",{"d":0},1],["RC"],["M",{"d":0},2],["M",{"d":0},3]]},"3":{"V":[["M",{"d":0},0],["QP",{"d":-2}],["QX",{"d":2}],["M",{"d":0},1],["M",{"d":0},2],["QC"],["M",{"d":0},3]]},"14":{"P":[["A",14,2],["B",14,0],["A",14,3],["B",14,1],["S3",10],["A",15,0],["B",14,2],["A",15,1],["B",14,3],["S3",11],["A",15,2],["B",15,0],["A",15,3],["S3",12],["B",15,1],["B",15,2],["B",15,3],["S3",13],["S3",14],["S3h",2],["S3h",3]],"S":[["C",14,2],["C",14,3],["O",10],["C",15,0],["C",15,1],["O",11],["C",15,2],["O",12],["C",15,3],["O",13],["O",14],["Oh",2]],"V":[["M",14,0],["QP",12],["M",14,1],["QP",13],["M",14,2],["M",14,3],["M",15,0],["M",15,1],["QP",14],["QPa",15],["M",15,2],["M",15,3],["QPc",15],["QPd",15],["Ohv",3]]},"15":{"P":[["NOP"]],"S":[["NOP"]],"V":[["NOP"]]}},"tail":{"P":[],"S":[],"V":[]},"vshare":[352,352,1],"pbf":4,"pq":6,"dma":[["w","a",0],["x","v",0,0,2],["w","b",0],["x","s",0,0,2],["x","v",0,2,4],["x","s",0,2,4],["x","v",1,0,2],["x","s",1,0,2],["w","a",1],["w","b",1],["x","v",1,2,4],["x","s",1,2,4],["c"]],"t3":3}
-NA = 3
-NB = 3
-NM = 2
-PERM = "vs"
-PFIRST = 6
+
+PAIRS = 16
+PHASES = 16
+A_BANKS, B_BANKS, MIX_BANKS = 3, 3, 2
+VSHARE = 88
+FIRST_REORDERED = 8
 
 
 def tile_vnclcell_pa_t_kernel(tc, v, s, Ca, Cb, Cc, out):
@@ -31,322 +31,297 @@ def tile_vnclcell_pa_t_kernel(tc, v, s, Ca, Cb, Cc, out):
         psum = ctx.enter_context(tc.psum_pool(name="psum", bufs=1))
         ctx.enter_context(tc.manual_schedule())
 
+        vcopy = nc.vector.tensor_copy
+        scopy = nc.scalar.copy
+
         ident = keep.tile([P, P], F32, name="ident")
         make_identity(nc, ident[:])
 
-        rows = {"v": v.rearrange("(p n) k -> p (n k)", n=NSUB), "s": s.rearrange("(p n) k -> p (n k)", n=NSUB)}
-        out_rows = out.rearrange("g (p n) h -> (g p) (n h)", n=NSUB)
-        wsrc = {"a": Ca, "b": Cb}
+        rows = {"v": v.rearrange("(p n) k -> p (n k)", n=ROWS), "s": s.rearrange("(p n) k -> p (n k)", n=ROWS)}
+        out_rows = out.rearrange("g (p n) h -> (g p) (n h)", n=ROWS)
+        weights = {"a": Ca, "b": Cb}
 
         x_in = {}
         for c in range(8):
             for x in "vs":
                 x_in[x, c] = keep.tile([P, 4 * K], BF16, name="x_%s%d" % (x, c))
-        w_raw = {}
-        w_q = {}
-        w_s = {}
+        w_raw, w_q, w_s = {}, {}, {}
         for w in "ab":
             for g in range(2):
-                w_raw[w, g] = keep.tile([P, 4, 512], BF16, name="raw_%s%d" % (w, g))
+                w_raw[w, g] = keep.tile([P, 4, HALF], BF16, name="raw_%s%d" % (w, g))
             w_q[w] = keep.tile([P, R], U32, name="wq_" + w, align_bytes=64)
             w_s[w] = keep.tile([P, R], U8, name="ws_" + w, align_bytes=64)
-        c_raw = keep.tile([P, 8, H], BF16, name="raw_c")
+        c_raw = keep.tile([P, 2, 4, H], BF16, name="raw_c")
         c_q = keep.tile([P, 2 * H], U32, name="cq", align_bytes=64)
         c_s = keep.tile([P, 2 * H], U8, name="cs", align_bytes=64)
 
-        def load_x(x, c, lo, hi):
-            nc.sync.dma_start(out=x_in[x, c][:, lo * K:hi * K], in_=rows[x][:, (4 * c + lo) * K:(4 * c + hi) * K])
+        def load_x(c, lo, hi, names="vs"):
+            for x in names:
+                nc.sync.dma_start(out=x_in[x, c][:, lo * K:hi * K], in_=rows[x][:, (4 * c + lo) * K:(4 * c + hi) * K])
 
         def load_w(w, g):
-            nc.sync.dma_start(out=w_raw[w, g][:], in_=wsrc[w][0, :, 512 * g:512 * g + 512].rearrange("(p j) c -> p j c", j=4))
+            nc.sync.dma_start(out=w_raw[w, g][:], in_=weights[w][0, :, HALF * g:HALF * g + HALF].rearrange("(p j) c -> p j c", j=4))
 
-        for item in SPEC["dma"]:
-            if item[0] == "w":
-                load_w(item[1], item[2])
-            elif item[0] == "x":
-                load_x(item[1], item[2], item[3], item[4])
-            else:
-                nc.sync.dma_start(out=c_raw[:, 0:4, :], in_=Cc[0, 0:512, :].rearrange("(p j) h -> p j h", j=4))
-                nc.sync.dma_start(out=c_raw[:, 4:8, :], in_=Cc[0, 512:1024, :].rearrange("(p j) h -> p j h", j=4))
+        load_w("a", 0)
+        load_x(0, 0, 2, "v")
+        load_w("b", 0)
+        load_x(0, 0, 2, "s")
+        load_x(0, 2, 4)
+        load_x(1, 0, 2)
+        load_w("a", 1)
+        load_w("b", 1)
+        load_x(1, 2, 4)
+        for g in range(2):
+            nc.sync.dma_start(out=c_raw[:, g], in_=Cc[0, 512 * g:512 * g + 512, :].rearrange("(p j) h -> p j h", j=4))
         for c in range(2, 8):
-            load_x("v", c, 0, 4)
-            load_x("s", c, 0, 4)
+            load_x(c, 0, 4)
 
-        def regroup(copy, dst, src):
-            copy(out=dst.rearrange("p (c i t) -> p c t i", i=4, t=4), in_=src.rearrange("p t (c i) -> p c t i", i=4))
+        grouped = {}
 
-        grp = {}
-
-        def w_regroup(w, g):
-            grp[w, g] = ring.tile([P, 2048], BF16, name="grp", tag="grp", bufs=3, align_bytes=64)
-            vs = SPEC["vshare"][g] // 4
-            dst = grp[w, g][:].rearrange("p (t m j) -> p m j t", t=4, j=4)
+        def regroup_w(w, g):
+            grouped[w, g] = ring.tile([P, 2048], BF16, name="grp", tag="grp", bufs=3, align_bytes=64)
+            dst = grouped[w, g][:].rearrange("p (t m j) -> p m j t", t=4, j=4)
             src = w_raw[w, g][:].rearrange("p j (m t) -> p m j t", t=4)
-            nc.vector.tensor_copy(out=dst[:, 0:vs], in_=src[:, 0:vs])
-            nc.scalar.copy(out=dst[:, vs:P], in_=src[:, vs:P])
+            vcopy(out=dst[:, 0:VSHARE], in_=src[:, 0:VSHARE])
+            scopy(out=dst[:, VSHARE:P], in_=src[:, VSHARE:P])
 
-        def w_quant(w, g):
-            nc.vector.quantize_mx(out=w_q[w][:, 512 * g:512 * g + 512].bitcast(FP8X4), scales=w_s[w][:, 512 * g:512 * g + 512],
-                                  in_=grp[w, g][:])
+        def quantize_w(w, g):
+            cols = slice(HALF * g, HALF * g + HALF)
+            nc.vector.quantize_mx(out=w_q[w][:, cols].bitcast(FP8X4), scales=w_s[w][:, cols], in_=grouped[w, g][:])
 
-        def c_regroup(copy):
-            grp["c"] = ring.tile([P, 2048], BF16, name="grp", tag="grp", bufs=3, align_bytes=64)
-            regroup(nc.vector.tensor_copy, grp["c"][:, 0:1024], c_raw[:, 0:4, :])
-            regroup(nc.vector.tensor_copy if SPEC["vshare"][2] else nc.scalar.copy, grp["c"][:, 1024:2048], c_raw[:, 4:8, :])
+        def regroup_c():
+            grouped["c"] = ring.tile([P, 2048], BF16, name="grp", tag="grp", bufs=3, align_bytes=64)
+            for g in range(2):
+                vcopy(out=grouped["c"][:, 1024 * g:1024 * g + 1024].rearrange("p (c i j) -> p c j i", i=4, j=4),
+                      in_=c_raw[:, g].rearrange("p j (c i) -> p c j i", i=4))
 
-        def c_quant():
-            nc.vector.quantize_mx(out=c_q[:].bitcast(FP8X4), scales=c_s[:], in_=grp["c"][:])
+        def quantize_c():
+            nc.vector.quantize_mx(out=c_q[:].bitcast(FP8X4), scales=c_s[:], in_=grouped["c"][:])
 
-        tb = {}
-        xg = {}
-        xq = {}
-        xs = {}
+        ordered = {}
+        turned = {}
+        x_grouped, x_q, x_s = {}, {}, {}
 
-        xp = {}
-
-        def PW(t):
-            c, hp = divmod(t, 2)
-            for x in PERM:
-                xp[x, t] = ring.tile([P, 1024], BF16, name="xp" + x, tag="xp" + x, bufs=3, align_bytes=64)
-                nc.gpsimd.tensor_copy(out=xp[x, t][:].bitcast(U32).rearrange("p (i u q) -> p i u q", i=2, u=2),
-                                      in_=x_in[x, c][:, 1024 * hp:1024 * hp + 1024].bitcast(U32).rearrange("p (i q u) -> p i u q", i=2, u=2))
-
-        def T(t):
-            c, hp = divmod(t, 2)
+        def reorder(t):
+            c, h = divmod(t, 2)
             for x in "vs":
-                tb[x, t] = psum.tile([P, 512], F32, name="tb", tag="m", bufs=NM)
-                words = x_in[x, c][:].bitcast(F32)
+                ordered[x, t] = ring.tile([P, 2 * K], BF16, name="ord_" + x, tag="ord_" + x, bufs=3, align_bytes=64)
+                nc.gpsimd.tensor_copy(out=ordered[x, t][:].bitcast(U32).rearrange("p (i u q) -> p i u q", i=2, u=2),
+                                      in_=x_in[x, c][:, 1024 * h:1024 * h + 1024].bitcast(U32).rearrange("p (i q u) -> p i u q", i=2, u=2))
+
+        def transpose(t):
+            c, h = divmod(t, 2)
+            for x in "vs":
+                turned[x, t] = psum.tile([P, 512], F32, name="turned", tag="mix", bufs=MIX_BANKS)
                 for u in range(2):
                     for i in range(2):
-                        if (x, t) in xp:
-                            w = xp[x, t][:].bitcast(F32)[:, 256 * i + 128 * u:256 * i + 128 * u + 128]
+                        if t >= FIRST_REORDERED:
+                            start = 256 * i + 128 * u
+                            words = ordered[x, t][:].bitcast(F32)[:, start:start + 128]
                         else:
-                            w = words[:, (2 * hp + i) * 256 + u:(2 * hp + i + 1) * 256:2]
-                        nc.tensor.transpose(tb[x, t][:, 256 * u + 128 * i:256 * u + 128 * i + 128], w, ident[:])
+                            start = 256 * (2 * h + i)
+                            words = x_in[x, c][:].bitcast(F32)[:, start + u:start + 256:2]
+                        nc.tensor.transpose(turned[x, t][:, 256 * u + 128 * i:256 * u + 128 * i + 128], words, ident[:])
+            if FIRST_REORDERED <= t < PAIRS - 3:
+                reorder(t + 3)
 
-        def X(t, x, copy):
+        def group_x(t, x):
             if x == "v":
-                xg[t] = ring.tile([P, 2048], BF16, name="xg", tag="xg", bufs=3, align_bytes=64)
+                x_grouped[t] = ring.tile([P, 2048], BF16, name="xg", tag="xg", bufs=3, align_bytes=64)
             o = 0 if x == "v" else 512
-            copy(out=xg[t][:].bitcast(F32)[:, o:o + 512].rearrange("p (c u) -> p c u", u=2),
-                 in_=tb[x, t][:].rearrange("p (u c) -> p c u", u=2))
+            scopy(out=x_grouped[t][:].bitcast(F32)[:, o:o + 512].rearrange("p (c u) -> p c u", u=2),
+                  in_=turned[x, t][:].rearrange("p (u c) -> p c u", u=2))
 
-        def QX(t):
-            xq[t] = ring.tile([P, 512], U32, name="xq", tag="xq", bufs=6, align_bytes=64)
-            xs[t] = ring.tile([P, 512], U8, name="xs", tag="xs", bufs=6, align_bytes=64)
-            nc.vector.quantize_mx(out=xq[t][:].bitcast(FP8X4), scales=xs[t][:], in_=xg[t][:])
+        def quantize_x(t):
+            x_q[t] = ring.tile([P, 512], U32, name="xq", tag="xq", bufs=6, align_bytes=64)
+            x_s[t] = ring.tile([P, 512], U8, name="xs", tag="xs", bufs=6, align_bytes=64)
+            nc.vector.quantize_mx(out=x_q[t][:].bitcast(FP8X4), scales=x_s[t][:], in_=x_grouped[t][:])
 
-        for t in range(PFIRST, PFIRST + 3):
-            PW(t)
+        t3_bank, t4_bank, t3, prod = {}, {}, {}, {}
 
-        bank = {}
-        t3 = {}
-        pbf = {}
-        pq = {}
-        ps = {}
+        def pair_of(f, i):
+            return 2 * (f // 2) + i // 2
 
-        def U(f, nl, which):
-            c, g = divmod(f, 2)
-            t, i = 2 * c + nl // 2, nl % 2
-            if which == "a":
-                bank["a", f, nl] = psum.tile([P, 512], F32, name="bka", tag="a", bufs=NA)
-                for jj in range(2):
-                    m = (4 * g + 2 * i + jj) * P
-                    nc.tensor.matmul_mx(out=bank["a", f, nl][:, jj * 256:(jj + 1) * 256],
-                                        lhsT=w_q["a"][:, m:m + P].bitcast(FP8X4), lhsT_scale=w_s["a"][:, m:m + P],
-                                        rhs=xq[t][:, 0:256].bitcast(FP8X4), rhs_scale=xs[t][:, 0:256],
-                                        start=True, stop=True)
-                return
-            for w, o, nb in (("b", 256, NB),):
-                bank[w, f, nl] = psum.tile([P, 512], F32, name="bk" + w, tag=w, bufs=nb)
-                for j in range(4):
-                    m = (4 * g + j) * P
-                    n = o + i * P
-                    nc.tensor.matmul_mx(out=bank[w, f, nl][:, j * P:(j + 1) * P],
-                                        lhsT=w_q[w][:, m:m + P].bitcast(FP8X4), lhsT_scale=w_s[w][:, m:m + P],
-                                        rhs=xq[t][:, n:n + P].bitcast(FP8X4), rhs_scale=xs[t][:, n:n + P],
-                                        start=True, stop=True)
+        def matmul_t3(f, i):
+            t = pair_of(f, i)
+            t3_bank[f, i] = psum.tile([P, 512], F32, name="t3b", tag="t3b", bufs=A_BANKS)
+            for e in range(2):
+                m = HALF * (f % 2) + P * (2 * (i % 2) + e)
+                nc.tensor.matmul_mx(out=t3_bank[f, i][:, 256 * e:256 * e + 256],
+                                    lhsT=w_q["a"][:, m:m + P].bitcast(FP8X4), lhsT_scale=w_s["a"][:, m:m + P],
+                                    rhs=x_q[t][:, 0:256].bitcast(FP8X4), rhs_scale=x_s[t][:, 0:256], start=True, stop=True)
 
-        def C(f, nl):
-            if nl % 2 == 0:
-                t3[f, nl // 2] = ring.tile([P, 2, 256, 2], F32, name="t3", tag="t3", bufs=SPEC.get("t3", 3))
-            nc.scalar.copy(out=t3[f, nl // 2][:, nl % 2, :, :], in_=bank["a", f, nl][:].rearrange("p (e w) -> p w e", e=2))
+        def matmul_t4(f, i):
+            t = pair_of(f, i)
+            n = 256 + P * (i % 2)
+            t4_bank[f, i] = psum.tile([P, 512], F32, name="t4b", tag="t4b", bufs=B_BANKS)
+            for j in range(4):
+                m = HALF * (f % 2) + P * j
+                nc.tensor.matmul_mx(out=t4_bank[f, i][:, P * j:P * j + P],
+                                    lhsT=w_q["b"][:, m:m + P].bitcast(FP8X4), lhsT_scale=w_s["b"][:, m:m + P],
+                                    rhs=x_q[t][:, n:n + P].bitcast(FP8X4), rhs_scale=x_s[t][:, n:n + P], start=True, stop=True)
 
-        def M(f, nl):
-            if nl == 0:
-                pbf[f] = ring.tile([P, 2048], BF16, name="pbf", tag="pbf", bufs=SPEC.get("pbf", 3), align_bytes=64)
-            nc.vector.tensor_tensor(out=pbf[f][:, 512 * nl:512 * nl + 512].rearrange("p (w h e) -> p w h e", h=2, e=2),
-                                    in0=bank["b", f, nl][:].rearrange("p (h e w) -> p w h e", h=2, e=2),
-                                    in1=t3[f, nl // 2][:, :, (nl % 2) * P:(nl % 2 + 1) * P, :].rearrange("p h w e -> p w h e"),
-                                    op=mybir.AluOpType.mult)
+        def copy_t3(f, i):
+            if i % 2 == 0:
+                t3[f, i // 2] = ring.tile([P, 2, 256, 2], F32, name="t3", tag="t3", bufs=3)
+            scopy(out=t3[f, i // 2][:, i % 2], in_=t3_bank[f, i][:].rearrange("p (e w) -> p w e", e=2))
 
-        def QP(f, lo=0, hi=4):
+        def multiply(f, i):
+            if i == 0:
+                prod[f] = ring.tile([P, 2048], BF16, name="prod", tag="prod", bufs=4, align_bytes=64)
+            w = P * (i % 2)
+            nc.vector.tensor_tensor(out=prod[f][:, 512 * i:512 * i + 512].rearrange("p (w h e) -> p w h e", h=2, e=2),
+                                    in0=t4_bank[f, i][:].rearrange("p (h e w) -> p w h e", h=2, e=2),
+                                    in1=t3[f, i // 2][:, :, w:w + P, :].rearrange("p h w e -> p w h e"), op=MULT)
+
+        prod_q, prod_s, out_bank = {}, {}, {}
+
+        def quantize_prod(f, lo=0, hi=4):
             if lo == 0:
-                pq[f] = ring.tile([P, 512], U32, name="pq", tag="pq", bufs=SPEC.get("pq", 6), align_bytes=64)
-                ps[f] = ring.tile([P, 512], U8, name="ps", tag="ps", bufs=SPEC.get("pq", 6), align_bytes=64)
-            nc.vector.quantize_mx(out=pq[f][:, P * lo:P * hi].bitcast(FP8X4), scales=ps[f][:, P * lo:P * hi],
-                                  in_=pbf[f][:, 512 * lo:512 * hi])
+                prod_q[f] = ring.tile([P, 512], U32, name="pq", tag="pq", bufs=6, align_bytes=64)
+                prod_s[f] = ring.tile([P, 512], U8, name="ps", tag="ps", bufs=6, align_bytes=64)
+            nc.vector.quantize_mx(out=prod_q[f][:, P * lo:P * hi].bitcast(FP8X4), scales=prod_s[f][:, P * lo:P * hi],
+                                  in_=prod[f][:, 512 * lo:512 * hi])
 
-        ob = {}
-        osb = {}
-
-        def S3(c, lo, hi, tag="m", nb=NM):
-            ob[c, lo] = psum.tile([P, 512], F32, name="ob", tag=tag, bufs=nb)
-            for nl in range(lo, hi):
+        def matmul_out(lo, hi):
+            out_bank[lo] = psum.tile([P, 512], F32, name="outb", tag="mix", bufs=MIX_BANKS)
+            for n in range(lo, hi):
+                c, i = divmod(n, 4)
                 for g in range(2):
-                    nc.tensor.matmul_mx(out=ob[c, lo][:, (nl - lo) * H:(nl - lo + 1) * H],
-                                        lhsT=pq[2 * c + g][:, nl * P:(nl + 1) * P].bitcast(FP8X4),
-                                        lhsT_scale=ps[2 * c + g][:, nl * P:(nl + 1) * P],
-                                        rhs=c_q[:, g * H:(g + 1) * H].bitcast(FP8X4), rhs_scale=c_s[:, g * H:(g + 1) * H],
+                    cols = slice(P * i, P * i + P)
+                    nc.tensor.matmul_mx(out=out_bank[lo][:, H * (n - lo):H * (n - lo) + H],
+                                        lhsT=prod_q[2 * c + g][:, cols].bitcast(FP8X4), lhsT_scale=prod_s[2 * c + g][:, cols],
+                                        rhs=c_q[:, H * g:H * g + H].bitcast(FP8X4), rhs_scale=c_s[:, H * g:H * g + H],
                                         start=(g == 0), stop=(g == 1))
 
-        def O(c, lo, hi, copy):
-            w = (hi - lo) * H
-            osb[c, lo] = ring.tile([P, 512], F32, name="osb", tag="osb", bufs=4)
-            copy(out=osb[c, lo][:, 0:w], in_=ob[c, lo][:, 0:w])
-            nc.sync.dma_start(out=out_rows[:, (4 * c + lo) * H:(4 * c + hi) * H], in_=osb[c, lo][:, 0:w])
+        def store(copy, lo, hi):
+            o = ring.tile([P, 512], F32, name="osb", tag="osb", bufs=4)
+            copy(out=o[:, 0:H * (hi - lo)], in_=out_bank[lo][:, 0:H * (hi - lo)])
+            nc.sync.dma_start(out=out_rows[:, H * lo:H * hi], in_=o[:, 0:H * (hi - lo)])
 
-        vcopy = nc.vector.tensor_copy
-        scopy = nc.scalar.copy
+        for t in range(FIRST_REORDERED, FIRST_REORDERED + 3):
+            reorder(t)
 
-        ops = {}
-        def add(key, eng, fn, pre):
-            ops[key] = (eng, fn, pre)
-        for w in "ab":
-            for g in range(2):
-                add(("RW", w, g), "VS", (lambda w=w, g=g: w_regroup(w, g)), [])
-                add(("QW", w, g), "V", (lambda w=w, g=g: w_quant(w, g)), [("RW", w, g)])
-        add(("RC",), "V", (lambda: c_regroup(vcopy)), [])
-        add(("QC",), "V", c_quant, [("RC",)])
-        for t in range(16):
-            add(("T", t), "P", (lambda t=t: (T(t), PW(t + 3) if PFIRST <= t <= 12 else 0)), [])
-            add(("Xv", t), "S", (lambda t=t: X(t, "v", scopy)), [("T", t)])
-            add(("Xs", t), "S", (lambda t=t: X(t, "s", scopy)), [("T", t), ("Xv", t)])
-            add(("QX", t), "V", (lambda t=t: QX(t)), [("Xs", t)])
-        for f in range(16):
-            c, g = divmod(f, 2)
-            for nl in range(4):
-                t = 2 * c + nl // 2
-                add(("A", f, nl), "P", (lambda f=f, nl=nl: U(f, nl, "a")), [("QX", t), ("QW", "a", g)])
-                add(("B", f, nl), "P", (lambda f=f, nl=nl: U(f, nl, "b")), [("QX", t), ("QW", "b", g)])
-                add(("C", f, nl), "S", (lambda f=f, nl=nl: C(f, nl)), [("A", f, nl)])
-                add(("M", f, nl), "V", (lambda f=f, nl=nl: M(f, nl)), [("C", f, 2 * (nl // 2)), ("C", f, 2 * (nl // 2) + 1), ("B", f, nl)] + ([("M", f, nl - 1)] if nl else []))
-            add(("QP", f), "V", (lambda f=f: QP(f)), [("M", f, 3)])
-            add(("QPa", f), "V", (lambda f=f: QP(f, 0, 2)), [("M", f, 1)])
-            add(("QPb", f), "V", (lambda f=f: QP(f, 2, 4)), [("M", f, 3), ("QPa", f)])
-            add(("QPc", f), "V", (lambda f=f: QP(f, 2, 3)), [("M", f, 2), ("QPa", f)])
-            add(("QPd", f), "V", (lambda f=f: QP(f, 3, 4)), [("M", f, 3), ("QPc", f)])
-        for q in range(16):
-            c = q // 2
-            add(("S3", q), "P", (lambda q=q: S3(q // 2, 2 * (q % 2), 2 * (q % 2) + 2)), [("QPx", 2 * c, q % 2), ("QPx", 2 * c + 1, q % 2), ("QC",)])
-            add(("O", q), "S", (lambda q=q: O(q // 2, 2 * (q % 2), 2 * (q % 2) + 2, scopy)), [("S3", q)])
-            add(("Ov", q), "V", (lambda q=q: O(q // 2, 2 * (q % 2), 2 * (q % 2) + 2, vcopy)), [("S3", q)])
-        for nl in (2, 3):
-            add(("S3h", nl), "P", (lambda nl=nl: S3(7, nl, nl + 1)), [("QPx", 14, 1), ("QPy", 15, nl), ("QC",)])
-            add(("Oh", nl), "S", (lambda nl=nl: O(7, nl, nl + 1, scopy)), [("S3h", nl)])
-            add(("Ohv", nl), "V", (lambda nl=nl: O(7, nl, nl + 1, vcopy)), [("S3h", nl)])
+        regroup_w("a", 0)
+        transpose(0)
+        group_x(0, "v")
+        regroup_w("b", 0)
+        group_x(0, "s")
+        quantize_w("a", 0)
+        quantize_x(0)
+        quantize_w("b", 0)
+        transpose(1)
+        group_x(1, "v")
+        group_x(1, "s")
+        matmul_t3(0, 0)
+        matmul_t3(0, 1)
+        copy_t3(0, 0)
+        copy_t3(0, 1)
 
-        def expand(seq, f):
-            res = []
-            for item in seq:
-                nm, args = item[0], item[1:]
-                key = tuple([nm] + [(f + a["d"] if isinstance(a, dict) else a) for a in args])
-                res.append(key)
-            return res
+        quantize_x(1)
+        matmul_t4(0, 0)
+        matmul_t4(0, 1)
+        matmul_t3(0, 2)
+        regroup_w("a", 1)
+        copy_t3(0, 2)
+        matmul_t3(0, 3)
+        copy_t3(0, 3)
+        transpose(2)
+        group_x(2, "v")
+        group_x(2, "s")
+        multiply(0, 0)
+        multiply(0, 1)
+        quantize_w("a", 1)
+        regroup_w("b", 1)
+        matmul_t4(0, 2)
+        multiply(0, 2)
+        quantize_x(2)
+        quantize_w("b", 1)
+        matmul_t4(0, 3)
+        matmul_t3(1, 0)
+        copy_t3(1, 0)
+        matmul_t3(1, 1)
+        copy_t3(1, 1)
+        multiply(0, 3)
 
-        queues = {"P": [], "S": [], "V": []}
-        for e in "PSV":
-            for key in SPEC["head"][e]:
-                queues[e].append(tuple(key))
-        for f in range(16):
-            for e in "PSV":
-                spec = SPEC["phase_special"].get(str(f), {}).get(e) or SPEC["phase"][e]
-                for key in expand(spec, f):
-                    if key[0] == "NOP": continue
-                    if key[0] in ("T", "Xv", "Xs", "QX") and not (0 <= key[1] < 16): continue
-                    if key[0] in ("S3", "O", "Ov") and not (0 <= key[1] < 16): continue
-                    if key[0] in ("QP", "A", "B", "C", "M") and not (0 <= key[1] < 16): continue
-                    queues[e].append(key)
-        for e in "PSV":
-            for key in SPEC["tail"][e]:
-                queues[e].append(tuple(key))
-        done = set()
+        for f in range(1, 14):
+            q = f - 4
+            transpose(f + 2)
+            group_x(f + 2, "v")
+            group_x(f + 2, "s")
+            matmul_t3(f, 2)
+            copy_t3(f, 2)
+            matmul_t4(f, 0)
+            multiply(f, 0)
+            if f == 1:
+                regroup_c()
+            matmul_t3(f, 3)
+            copy_t3(f, 3)
+            matmul_t4(f, 1)
+            multiply(f, 1)
+            if q >= 0:
+                matmul_out(2 * q, 2 * q + 2)
+                store(vcopy if q % 4 == 3 else scopy, 2 * q, 2 * q + 2)
+            quantize_x(f + 2)
+            if f >= 2:
+                quantize_prod(f - 2)
+            matmul_t3(f + 1, 0)
+            copy_t3(f + 1, 0)
+            matmul_t4(f, 2)
+            multiply(f, 2)
+            if f == 3:
+                quantize_c()
+            matmul_t3(f + 1, 1)
+            copy_t3(f + 1, 1)
+            matmul_t4(f, 3)
+            multiply(f, 3)
 
-        def sat(p):
-            if p[0] == "QPx":
-                return ("QP", p[1]) in done or (("QPa", p[1]) in done if p[2] == 0 else (("QPb", p[1]) in done or ("QPd", p[1]) in done))
-            if p[0] == "QPy":
-                return ("QP", p[1]) in done or ("QPb", p[1]) in done or (("QPc", p[1]) in done if p[2] == 2 else ("QPd", p[1]) in done)
-            if p[0] == "Oany":
-                return ("O", p[1]) in done or ("Ov", p[1]) in done
-            if p[0] == "Ohany":
-                return ("Oh", p[1]) in done or ("Ohv", p[1]) in done
-            return p in done
+        matmul_t3(14, 2)
+        copy_t3(14, 2)
+        matmul_t4(14, 0)
+        multiply(14, 0)
+        quantize_prod(12)
+        matmul_t3(14, 3)
+        copy_t3(14, 3)
+        matmul_t4(14, 1)
+        multiply(14, 1)
+        quantize_prod(13)
+        matmul_out(20, 22)
+        store(scopy, 20, 22)
+        matmul_t3(15, 0)
+        copy_t3(15, 0)
+        matmul_t4(14, 2)
+        multiply(14, 2)
+        matmul_t3(15, 1)
+        copy_t3(15, 1)
+        matmul_t4(14, 3)
+        multiply(14, 3)
 
-        m_readers = []
-        grp_users = []
-
-        def reuse(key):
-            k = key[0]
-            res = []
-            if k in ("A", "B", "C"):
-                n = 4 * key[1] + key[2]
-                back = {"A": NA, "B": NB, "C": 2 * SPEC.get("t3", 3) - 1}[k]
-                if k == "C" and n % 2 == 1:
-                    back = n + 1
-                if n - back >= 0:
-                    res.append(({"A": "C", "B": "M", "C": "M"}[k], (n - back) // 4, (n - back) % 4))
-            if k in ("T", "S3", "S3h"):
-                need = 2 if k == "T" else 1
-                for i in range(need):
-                    j = len(m_readers) + i - NM
-                    if j >= 0:
-                        res.append(m_readers[j] if j < len(m_readers) else ("never",))
-            if k == "Xv" and key[1] >= 3:
-                res.append(("QX", key[1] - 3))
-            if k == "QX" and key[1] >= 6:
-                t = key[1] - 6
-                res.append(("B", 2 * (t // 2) + 1, 2 * (t % 2) + 1))
-            if k == "M" and key[2] == 0 and key[1] >= SPEC.get("pbf", 3):
-                res.append(("QPx", key[1] - SPEC.get("pbf", 3), 1))
-            if k in ("QP", "QPa") and key[1] >= SPEC.get("pq", 6):
-                res.append(("S3", 2 * ((key[1] - SPEC.get("pq", 6)) // 2) + 1))
-            if k in ("RW", "RC") and len(grp_users) >= 3:
-                res.append(grp_users[len(grp_users) - 3])
-            return res
-
-        def emitted(key):
-            k = key[0]
-            if k == "T":
-                m_readers.append(("Xv", key[1]))
-                m_readers.append(("Xs", key[1]))
-            if k == "S3":
-                m_readers.append(("Oany", key[1]))
-            if k == "S3h":
-                m_readers.append(("Ohany", key[1]))
-            if k == "RW":
-                grp_users.append(("QW", key[1], key[2]))
-            if k == "RC":
-                grp_users.append(("QC",))
-            done.add(key)
-
-        pos = {"P": 0, "S": 0, "V": 0}
-        while any(pos[e] < len(queues[e]) for e in "PSV"):
-            prog = False
-            for e in "PSV":
-                if pos[e] >= len(queues[e]):
-                    continue
-                key = queues[e][pos[e]]
-                eng, fn, prq = ops[key]
-                if not all(sat(p) for p in list(prq) + reuse(key)):
-                    continue
-                if key[0] == "RW" or (key[0] == "RC" and not SPEC["vshare"][2]):
-                    other = "S" if e == "V" else "V"
-                    if not (pos[other] < len(queues[other]) and queues[other][pos[other]] == key):
-                        continue
-                    pos[other] += 1
-                fn()
-                emitted(key)
-                pos[e] += 1
-                prog = True
-            assert prog, "the three orders cannot be merged"
+        matmul_out(22, 24)
+        store(scopy, 22, 24)
+        matmul_t3(15, 2)
+        copy_t3(15, 2)
+        matmul_t4(15, 0)
+        multiply(15, 0)
+        matmul_t3(15, 3)
+        matmul_out(24, 26)
+        store(scopy, 24, 26)
+        copy_t3(15, 3)
+        matmul_t4(15, 1)
+        multiply(15, 1)
+        matmul_t4(15, 2)
+        quantize_prod(14)
+        quantize_prod(15, 0, 2)
+        multiply(15, 2)
+        matmul_t4(15, 3)
+        matmul_out(26, 28)
+        store(scopy, 26, 28)
+        multiply(15, 3)
+        quantize_prod(15, 2, 3)
+        quantize_prod(15, 3, 4)
+        matmul_out(28, 30)
+        store(scopy, 28, 30)
+        matmul_out(30, 31)
+        store(scopy, 30, 31)
+        matmul_out(31, 32)
+        store(vcopy, 31, 32)

@@ -20,6 +20,7 @@ PAIRS = 16
 PHASES = 16
 A_BANKS, B_BANKS, MIX_BANKS = 3, 3, 2
 VSHARE = 88
+C_PIECE = 64
 FIRST_REORDERED = 8
 
 
@@ -91,9 +92,10 @@ def tile_vnclcell_pa_t_kernel(tc, v, s, Ca, Cb, Cc, out):
 
         def regroup_c():
             grouped["c"] = ring.tile([P, 2048], BF16, name="grp", tag="grp", bufs=3, align_bytes=64)
+            dst = grouped["c"][:].rearrange("p (g c j) -> p g c j", g=2, j=4)
             for g in range(2):
-                vcopy(out=grouped["c"][:, 1024 * g:1024 * g + 1024].rearrange("p (c i j) -> p c j i", i=4, j=4),
-                      in_=c_raw[:, g].rearrange("p j (c i) -> p c j i", i=4))
+                for lo in range(0, H, C_PIECE):
+                    nc.gpsimd.tensor_copy(out=dst[:, g, lo:lo + C_PIECE], in_=c_raw[:, g, :, lo:lo + C_PIECE].rearrange("p j c -> p c j"))
 
         def quantize_c():
             nc.vector.quantize_mx(out=c_q[:].bitcast(FP8X4), scales=c_s[:], in_=grouped["c"][:])
@@ -199,8 +201,6 @@ def tile_vnclcell_pa_t_kernel(tc, v, s, Ca, Cb, Cc, out):
             copy(out=o[:, 0:H * (hi - lo)], in_=out_bank[lo][:, 0:H * (hi - lo)])
             nc.sync.dma_start(out=out_rows[:, H * lo:H * hi], in_=o[:, 0:H * (hi - lo)])
 
-        for t in range(FIRST_REORDERED, FIRST_REORDERED + 3):
-            reorder(t)
 
         regroup_w("a", 0)
         transpose(0)
@@ -244,6 +244,10 @@ def tile_vnclcell_pa_t_kernel(tc, v, s, Ca, Cb, Cc, out):
         copy_t3(1, 1)
         multiply(0, 3)
 
+        regroup_c()
+        for t in range(FIRST_REORDERED, FIRST_REORDERED + 3):
+            reorder(t)
+
         for f in range(1, 14):
             q = f - 4
             transpose(f + 2)
@@ -253,15 +257,13 @@ def tile_vnclcell_pa_t_kernel(tc, v, s, Ca, Cb, Cc, out):
             copy_t3(f, 2)
             matmul_t4(f, 0)
             multiply(f, 0)
-            if f == 1:
-                regroup_c()
             matmul_t3(f, 3)
             copy_t3(f, 3)
             matmul_t4(f, 1)
             multiply(f, 1)
             if q >= 0:
                 matmul_out(2 * q, 2 * q + 2)
-                store(vcopy if q % 4 == 3 else scopy, 2 * q, 2 * q + 2)
+                store(scopy, 2 * q, 2 * q + 2)
             quantize_x(f + 2)
             if f >= 2:
                 quantize_prod(f - 2)

@@ -21,7 +21,7 @@ PHASES = 16
 A_BANKS, B_BANKS, MIX_BANKS = 3, 3, 2
 VSHARE = 88
 C_PIECE = 64
-FIRST_REORDERED = 8
+FIRST_REORDERED = 7
 
 
 def tile_vnclcell_pa_t_kernel(tc, v, s, Ca, Cb, Cc, out):
@@ -64,9 +64,8 @@ def tile_vnclcell_pa_t_kernel(tc, v, s, Ca, Cb, Cc, out):
             nc.sync.dma_start(out=w_raw[w, g][:], in_=weights[w][0, :, HALF * g:HALF * g + HALF].rearrange("(p j) c -> p j c", j=4))
 
         load_w("a", 0)
-        load_x(0, 0, 2, "v")
+        load_x(0, 0, 2)
         load_w("b", 0)
-        load_x(0, 0, 2, "s")
         load_x(0, 2, 4)
         load_x(1, 0, 2)
         load_w("a", 1)
@@ -108,8 +107,10 @@ def tile_vnclcell_pa_t_kernel(tc, v, s, Ca, Cb, Cc, out):
             c, h = divmod(t, 2)
             for x in "vs":
                 ordered[x, t] = ring.tile([P, 2 * K], BF16, name="ord_" + x, tag="ord_" + x, bufs=3, align_bytes=64)
-                nc.gpsimd.tensor_copy(out=ordered[x, t][:].bitcast(U32).rearrange("p (i u q) -> p i u q", i=2, u=2),
-                                      in_=x_in[x, c][:, 1024 * h:1024 * h + 1024].bitcast(U32).rearrange("p (i q u) -> p i u q", i=2, u=2))
+                for i in range(2):
+                    row = K * (2 * h + i)
+                    nc.gpsimd.tensor_copy(out=ordered[x, t][:, K * i:K * i + K].bitcast(U32).rearrange("p (u q) -> p u q", u=2),
+                                          in_=x_in[x, c][:, row:row + K].bitcast(U32).rearrange("p (q u) -> p u q", u=2))
 
         def transpose(t):
             c, h = divmod(t, 2)
@@ -205,9 +206,9 @@ def tile_vnclcell_pa_t_kernel(tc, v, s, Ca, Cb, Cc, out):
         regroup_w("a", 0)
         transpose(0)
         group_x(0, "v")
-        regroup_w("b", 0)
         group_x(0, "s")
         quantize_w("a", 0)
+        regroup_w("b", 0)
         quantize_x(0)
         quantize_w("b", 0)
         transpose(1)

@@ -37,6 +37,8 @@ def tile_vnclcell_pa_t_kernel(tc, v, s, Ca, Cb, Cc, out):
 
         ident = keep.tile([P, P], F32, name="ident")
         make_identity(nc, ident[:])
+        zeros = keep.tile([P, 512], BF16, name="zeros")
+        nc.vector.memset(zeros[:], 0.0)
 
         rows = {"v": v.rearrange("(p n) k -> p (n k)", n=ROWS), "s": s.rearrange("(p n) k -> p (n k)", n=ROWS)}
         out_rows = out.rearrange("g (p n) h -> (g p) (n h)", n=ROWS)
@@ -67,8 +69,8 @@ def tile_vnclcell_pa_t_kernel(tc, v, s, Ca, Cb, Cc, out):
         load_x(0, 0, 2)
         load_w("b", 0)
         load_x(0, 2, 4)
-        load_x(1, 0, 2)
         load_w("a", 1)
+        load_x(1, 0, 2)
         load_w("b", 1)
         load_x(1, 2, 4)
         for g in range(2):
@@ -98,6 +100,11 @@ def tile_vnclcell_pa_t_kernel(tc, v, s, Ca, Cb, Cc, out):
 
         def quantize_c():
             nc.vector.quantize_mx(out=c_q[:].bitcast(FP8X4), scales=c_s[:], in_=grouped["c"][:])
+
+        def keep_clock(n):
+            for k in range(n):
+                idle = psum.tile([P, 512], F32, name="t4b", tag="t4b", bufs=B_BANKS)
+                nc.tensor.matmul(idle[:], lhsT=zeros[:, 0:P], rhs=zeros[:], start=True, stop=True)
 
         ordered = {}
         turned = {}
@@ -203,8 +210,10 @@ def tile_vnclcell_pa_t_kernel(tc, v, s, Ca, Cb, Cc, out):
             nc.sync.dma_start(out=out_rows[:, H * lo:H * hi], in_=o[:, 0:H * (hi - lo)])
 
 
+        keep_clock(6)
         regroup_w("a", 0)
         transpose(0)
+        keep_clock(3)
         group_x(0, "v")
         group_x(0, "s")
         quantize_w("a", 0)
@@ -214,6 +223,7 @@ def tile_vnclcell_pa_t_kernel(tc, v, s, Ca, Cb, Cc, out):
         transpose(1)
         group_x(1, "v")
         group_x(1, "s")
+        keep_clock(2)
         matmul_t3(0, 0)
         matmul_t3(0, 1)
         copy_t3(0, 0)

@@ -261,6 +261,8 @@ def tile_vnclcell_pa_t_kernel(tc, v, s, Ca, Cb, Cc, out):
 
         for f in range(1, 14):
             q = f - 4
+            if f >= 2:
+                quantize_prod(f - 2)
             transpose(f + 2)
             group_x(f + 2, "v")
             group_x(f + 2, "s")
@@ -274,10 +276,8 @@ def tile_vnclcell_pa_t_kernel(tc, v, s, Ca, Cb, Cc, out):
             multiply(f, 1)
             if q >= 0:
                 matmul_out(2 * q, 2 * q + 2)
-                store(scopy, 2 * q, 2 * q + 2)
+                store(vcopy if q % 4 == 3 else scopy, 2 * q, 2 * q + 2)
             quantize_x(f + 2)
-            if f >= 2:
-                quantize_prod(f - 2)
             matmul_t3(f + 1, 0)
             copy_t3(f + 1, 0)
             matmul_t4(f, 2)

from contextlib import ExitStack

import concourse.mybir as mybir
from concourse.masks import make_identity

F32 = mybir.dt.float32
BF16 = mybir.dt.bfloat16
U8 = mybir.dt.uint8
U32 = mybir.dt.uint32
FP8X4 = mybir.dt.float8_e4m3fn_x4
MULT = mybir.AluOpType.mult

P = 128
B, K, R, H = 4096, 512, 1024, 256
ROWS = B // P
HALF = 512
FLOPS = 2 * B * (2 * K * R + R * H)

PAIRS = 16
PHASES = 16
A_BANKS, B_BANKS, MIX_BANKS = 3, 3, 2
VSHARE = 88
C_PIECE = 64
FIRST_REORDERED = 7


def tile_vnclcell_pa_t_kernel(tc, v, s, Ca, Cb, Cc, out):
    nc = tc.nc
    with ExitStack() as ctx:
        keep = ctx.enter_context(tc.tile_pool(name="keep", bufs=1))
        ring = ctx.enter_context(tc.tile_pool(name="ring", bufs=2))
        psum = ctx.enter_context(tc.psum_pool(name="psum", bufs=1))
        ctx.enter_context(tc.manual_schedule())

        vcopy = nc.vector.tensor_copy
        scopy = nc.scalar.copy

        ident = keep.tile([P, P], F32, name="ident")
        make_identity(nc, ident[:])
        zeros = keep.tile([P, 512], BF16, name="zeros")
        nc.vector.memset(zeros[:], 0.0)

        rows = {"v": v.rearrange("(p n) k -> p (n k)", n=ROWS), "s": s.rearrange("(p n) k -> p (n k)", n=ROWS)}
        out_rows = out.rearrange("g (p n) h -> (g p) (n h)", n=ROWS)
        weights = {"a": Ca, "b": Cb}

        x_in = {}
        for c in range(8):
            for x in "vs":
                x_in[x, c] = keep.tile([P, 4 * K], BF16, name="x_%s%d" % (x, c))
        w_raw, w_q, w_s = {}, {}, {}
        for w in "ab":
            for g in range(2):
                w_raw[w, g] = keep.tile([P, 4, HALF], BF16, name="raw_%s%d" % (w, g))
            w_q[w] = keep.tile([P, R], U32, name="wq_" + w, align_bytes=64)
            w_s[w] = keep.tile([P, R], U8, name="ws_" + w, align_bytes=64)
        c_raw = keep.tile([P, 2, 4, H], BF16, name="raw_c")
        c_q = keep.tile([P, 2 * H], U32, name="cq", align_bytes=64)
        c_s = keep.tile([P, 2 * H], U8, name="cs", align_bytes=64)

        def load_x(c, lo, hi, names="vs"):
            for x in names:
                nc.sync.dma_start(out=x_in[x, c][:, lo * K:hi * K], in_=rows[x][:, (4 * c + lo) * K:(4 * c + hi) * K])

        def load_w(w, g):
            nc.sync.dma_start(out=w_raw[w, g][:], in_=weights[w][0, :, HALF * g:HALF * g + HALF].rearrange("(p j) c -> p j c", j=4))

        load_w("a", 0)
        load_x(0, 0, 2)
        load_w("b", 0)
        load_x(0, 2, 4)
        load_w("a", 1)
        load_x(1, 0, 2)
        load_w("b", 1)
        load_x(1, 2, 4)
        for g in range(2):
            nc.sync.dma_start(out=c_raw[:, g], in_=Cc[0, 512 * g:512 * g + 512, :].rearrange("(p j) h -> p j h", j=4))
        for c in range(2, 8):
            load_x(c, 0, 4)

        grouped = {}

        def regroup_w(w, g):
            grouped[w, g] = ring.tile([P, 2048], BF16, name="grp", tag="grp", bufs=3, align_bytes=64)
            dst = grouped[w, g][:].rearrange("p (t m j) -> p m j t", t=4, j=4)
            src = w_raw[w, g][:].rearrange("p j (m t) -> p m j t", t=4)
            vcopy(out=dst[:, 0:VSHARE], in_=src[:, 0:VSHARE])
            scopy(out=dst[:, VSHARE:P], in_=src[:, VSHARE:P])

        def quantize_w(w, g):
            cols = slice(HALF * g, HALF * g + HALF)
            nc.vector.quantize_mx(out=w_q[w][:, cols].bitcast(FP8X4), scales=w_s[w][:, cols], in_=grouped[w, g][:])

        def regroup_c():
            grouped["c"] = ring.tile([P, 2048], BF16, name="grp", tag="grp", bufs=3, align_bytes=64)
            dst = grouped["c"][:].rearrange("p (g c j) -> p g c j", g=2, j=4)
            for g in range(2):
                for lo in range(0, H, C_PIECE):
                    nc.gpsimd.tensor_copy(out=dst[:, g, lo:lo + C_PIECE], in_=c_raw[:, g, :, lo:lo + C_PIECE].rearrange("p j c -> p c j"))

        def quantize_c():
            nc.vector.quantize_mx(out=c_q[:].bitcast(FP8X4), scales=c_s[:], in_=grouped["c"][:])

        def keep_clock(n):
            for k in range(n):
                idle = psum.tile([P, 512], F32, name="t4b", tag="t4b", bufs=B_BANKS)
                nc.tensor.matmul(idle[:], lhsT=zeros[:, 0:P], rhs=zeros[:], start=True, stop=True)

        ordered = {}
        turned = {}
        x_grouped, x_q, x_s = {}, {}, {}

        def reorder(t):
            c, h = divmod(t, 2)
            for x in "vs":
                ordered[x, t] = ring.tile([P, 2 * K], BF16, name="ord_" + x, tag="ord_" + x, bufs=3, align_bytes=64)
                for i in range(2):
                    row = K * (2 * h + i)
                    nc.gpsimd.tensor_copy(out=ordered[x, t][:, K * i:K * i + K].bitcast(U32).rearrange("p (u q) -> p u q", u=2),
                                          in_=x_in[x, c][:, row:row + K].bitcast(U32).rearrange("p (q u) -> p u q", u=2))

        def transpose(t):
            c, h = divmod(t, 2)
            for x in "vs":
                turned[x, t] = psum.tile([P, 512], F32, name="turned", tag="mix", bufs=MIX_BANKS)
                for u in range(2):
                    for i in range(2):
                        if t >= FIRST_REORDERED:
                            start = 256 * i + 128 * u
                            words = ordered[x, t][:].bitcast(F32)[:, start:start + 128]
                        else:
                            start = 256 * (2 * h + i)
                            words = x_in[x, c][:].bitcast(F32)[:, start + u:start + 256:2]
                        nc.tensor.transpose(turned[x, t][:, 256 * u + 128 * i:256 * u + 128 * i + 128], words, ident[:])
            if FIRST_REORDERED <= t < PAIRS - 3:
                reorder(t + 3)

        def group_x(t, x):
            if x == "v":
                x_grouped[t] = ring.tile([P, 2048], BF16, name="xg", tag="xg", bufs=3, align_bytes=64)
            o = 0 if x == "v" else 512
            scopy(out=x_grouped[t][:].bitcast(F32)[:, o:o + 512].rearrange("p (c u) -> p c u", u=2),
                  in_=turned[x, t][:].rearrange("p (u c) -> p c u", u=2))

        def quantize_x(t):
            x_q[t] = ring.tile([P, 512], U32, name="xq", tag="xq", bufs=6, align_bytes=64)
            x_s[t] = ring.tile([P, 512], U8, name="xs", tag="xs", bufs=6, align_bytes=64)
            nc.vector.quantize_mx(out=x_q[t][:].bitcast(FP8X4), scales=x_s[t][:], in_=x_grouped[t][:])

        t3_bank, t4_bank, t3, prod = {}, {}, {}, {}

        def pair_of(f, i):
            return 2 * (f // 2) + i // 2

        def matmul_t3(f, i):
            t = pair_of(f, i)
            t3_bank[f, i] = psum.tile([P, 512], F32, name="t3b", tag="t3b", bufs=A_BANKS)
            for e in range(2):
                m = HALF * (f % 2) + P * (2 * (i % 2) + e)
                nc.tensor.matmul_mx(out=t3_bank[f, i][:, 256 * e:256 * e + 256],
                                    lhsT=w_q["a"][:, m:m + P].bitcast(FP8X4), lhsT_scale=w_s["a"][:, m:m + P],
                                    rhs=x_q[t][:, 0:256].bitcast(FP8X4), rhs_scale=x_s[t][:, 0:256], start=True, stop=True)

        def matmul_t4(f, i):
            t = pair_of(f, i)
            n = 256 + P * (i % 2)
            t4_bank[f, i] = psum.tile([P, 512], F32, name="t4b", tag="t4b", bufs=B_BANKS)
            for j in range(4):
                m = HALF * (f % 2) + P * j
                nc.tensor.matmul_mx(out=t4_bank[f, i][:, P * j:P * j + P],
                                    lhsT=w_q["b"][:, m:m + P].bitcast(FP8X4), lhsT_scale=w_s["b"][:, m:m + P],
                                    rhs=x_q[t][:, n:n + P].bitcast(FP8X4), rhs_scale=x_s[t][:, n:n + P], start=True, stop=True)

        def copy_t3(f, i):
            if i % 2 == 0:
                t3[f, i // 2] = ring.tile([P, 2, 256, 2], F32, name="t3", tag="t3", bufs=3)
            scopy(out=t3[f, i // 2][:, i % 2], in_=t3_bank[f, i][:].rearrange("p (e w) -> p w e", e=2))

        def multiply(f, i):
            if i == 0:
                prod[f] = ring.tile([P, 2048], BF16, name="prod", tag="prod", bufs=4, align_bytes=64)
            w = P * (i % 2)
            nc.vector.tensor_tensor(out=prod[f][:, 512 * i:512 * i + 512].rearrange("p (w h e) -> p w h e", h=2, e=2),
                                    in0=t4_bank[f, i][:].rearrange("p (h e w) -> p w h e", h=2, e=2),
                                    in1=t3[f, i // 2][:, :, w:w + P, :].rearrange("p h w e -> p w h e"), op=MULT)

        prod_q, prod_s, out_bank = {}, {}, {}

        def quantize_prod(f, lo=0, hi=4):
            if lo == 0:
                prod_q[f] = ring.tile([P, 512], U32, name="pq", tag="pq", bufs=6, align_bytes=64)
                prod_s[f] = ring.tile([P, 512], U8, name="ps", tag="ps", bufs=6, align_bytes=64)
            nc.vector.quantize_mx(out=prod_q[f][:, P * lo:P * hi].bitcast(FP8X4), scales=prod_s[f][:, P * lo:P * hi],
                                  in_=prod[f][:, 512 * lo:512 * hi])

        def matmul_out(lo, hi):
            out_bank[lo] = psum.tile([P, 512], F32, name="outb", tag="mix", bufs=MIX_BANKS)
            for n in range(lo, hi):
                c, i = divmod(n, 4)
                for g in range(2):
                    cols = slice(P * i, P * i + P)
                    nc.tensor.matmul_mx(out=out_bank[lo][:, H * (n - lo):H * (n - lo) + H],
                                        lhsT=prod_q[2 * c + g][:, cols].bitcast(FP8X4), lhsT_scale=prod_s[2 * c + g][:, cols],
                                        rhs=c_q[:, H * g:H * g + H].bitcast(FP8X4), rhs_scale=c_s[:, H * g:H * g + H],
                                        start=(g == 0), stop=(g == 1))

        def store(copy, lo, hi):
            o = ring.tile([P, 512], F32, name="osb", tag="osb", bufs=4)
            copy(out=o[:, 0:H * (hi - lo)], in_=out_bank[lo][:, 0:H * (hi - lo)])
            nc.sync.dma_start(out=out_rows[:, H * lo:H * hi], in_=o[:, 0:H * (hi - lo)])


        keep_clock(6)
        regroup_w("a", 0)
        transpose(0)
        keep_clock(3)
        group_x(0, "v")
        group_x(0, "s")
        quantize_w("a", 0)
        regroup_w("b", 0)
        quantize_x(0)
        quantize_w("b", 0)
        transpose(1)
        group_x(1, "v")
        group_x(1, "s")
        keep_clock(2)
        matmul_t3(0, 0)
        matmul_t3(0, 1)
        copy_t3(0, 0)
        copy_t3(0, 1)

        quantize_x(1)
        matmul_t4(0, 0)
        matmul_t4(0, 1)
        matmul_t3(0, 2)
        regroup_w("a", 1)
        copy_t3(0, 2)
        matmul_t3(0, 3)
        copy_t3(0, 3)
        transpose(2)
        group_x(2, "v")
        group_x(2, "s")
        multiply(0, 0)
        multiply(0, 1)
        quantize_w("a", 1)
        regroup_w("b", 1)
        matmul_t4(0, 2)
        multiply(0, 2)
        quantize_x(2)
        quantize_w("b", 1)
        matmul_t4(0, 3)
        matmul_t3(1, 0)
        copy_t3(1, 0)
        matmul_t3(1, 1)
        copy_t3(1, 1)
        multiply(0, 3)

        regroup_c()
        for t in range(FIRST_REORDERED, FIRST_REORDERED + 3):
            reorder(t)

        for f in range(1, 14):
            q = f - 4
            if f >= 2:
                quantize_prod(f - 2)
            transpose(f + 2)
            group_x(f + 2, "v")
            group_x(f + 2, "s")
            matmul_t3(f, 2)
            copy_t3(f, 2)
            matmul_t4(f, 0)
            multiply(f, 0)
            matmul_t3(f, 3)
            copy_t3(f, 3)
            matmul_t4(f, 1)
            multiply(f, 1)
            if q >= 0:
                matmul_out(2 * q, 2 * q + 2)
                store(vcopy if q % 4 == 3 else scopy, 2 * q, 2 * q + 2)
            quantize_x(f + 2)
            matmul_t3(f + 1, 0)
            copy_t3(f + 1, 0)
            matmul_t4(f, 2)
            multiply(f, 2)
            if f == 3:
                quantize_c()
            matmul_t3(f + 1, 1)
            copy_t3(f + 1, 1)
            matmul_t4(f, 3)
            multiply(f, 3)

        matmul_t3(14, 2)
        copy_t3(14, 2)
        matmul_t4(14, 0)
        multiply(14, 0)
        quantize_prod(12)
        matmul_t3(14, 3)
        copy_t3(14, 3)
        matmul_t4(14, 1)
        multiply(14, 1)
        quantize_prod(13)
        matmul_out(20, 22)
        store(scopy, 20, 22)
        matmul_t3(15, 0)
        copy_t3(15, 0)
        matmul_t4(14, 2)
        multiply(14, 2)
        matmul_t3(15, 1)
        copy_t3(15, 1)
        matmul_t4(14, 3)
        multiply(14, 3)

        matmul_out(22, 24)
        store(scopy, 22, 24)
        matmul_t3(15, 2)
        copy_t3(15, 2)
        matmul_t4(15, 0)
        multiply(15, 0)
        matmul_t3(15, 3)
        matmul_out(24, 26)
        store(scopy, 24, 26)
        copy_t3(15, 3)
        matmul_t4(15, 1)
        multiply(15, 1)
        matmul_t4(15, 2)
        quantize_prod(14)
        quantize_prod(15, 0, 2)
        multiply(15, 2)
        matmul_t4(15, 3)
        matmul_out(26, 28)
        store(scopy, 26, 28)
        multiply(15, 3)
        quantize_prod(15, 2, 3)
        quantize_prod(15, 3, 4)
        matmul_out(28, 30)
        store(scopy, 28, 30)
        matmul_out(30, 31)
        store(scopy, 30, 31)
        matmul_out(31, 32)
        store(vcopy, 31, 32)
